import numpy as np
import ml_dtypes


def mxq(x, axis, fmt="e4m3"):
    dtype, down = {"e4m3": (ml_dtypes.float8_e4m3fn, 7), "e5m2": (ml_dtypes.float8_e5m2, 14)}[fmt]
    v = np.moveaxis(np.asarray(x, np.float32).astype(ml_dtypes.bfloat16).astype(np.float64), axis, -1)
    blocks = v.reshape(v.shape[:-1] + (-1, 32))
    amax = np.abs(blocks).max(-1, keepdims=True)
    byte = np.maximum(np.where(amax > 0, np.frexp(amax)[1] - 1 + 127, 0) - down, 1)
    scale = np.exp2(byte - 127.0)
    codes = (blocks / scale).astype(np.float32).astype(dtype).astype(np.float64)
    return np.moveaxis((codes * scale).reshape(v.shape), -1, axis)


WIDE = False


def mx_kscale(k):
    if not WIDE:
        return np.ones(k)
    levels = np.array([10, -10, 5, -5, 0])
    a = np.random.permutation(np.resize(levels, k // 512 * 4)).reshape(k // 512, 4)
    idx = np.arange(k)
    return np.exp2(a[idx // 512, idx % 128 // 32])


BF16 = ml_dtypes.bfloat16


def bf(x):
    return np.asarray(x, np.float32).astype(BF16)


def f64(x):
    return np.asarray(x).astype(np.float64)


N, L, D, M = 1024, 4, 1024, 1024


def l2norm(v):
    n = np.sqrt((v * v).sum(axis=-1, keepdims=True))
    return v / np.maximum(n, 1e-12)


def setup_inputs():
    s = mx_kscale(D)
    amp_f = 0.5 + 1.5 * np.random.random((N, L))[:, :, None]
    amp_v = 0.5 + 1.5 * np.random.random(N)[:, None]
    return {"feature": bf(np.random.standard_normal((N, L, D)) * amp_f * s),
            "aspect_v": bf(np.random.standard_normal((N, D)) * amp_v * s),
            "W": bf(np.random.standard_normal((M, D)) * np.sqrt(2.0 / (D + M)) / s),
            "b": bf(np.random.standard_normal(M) * 0.2)}


def reference(feature, aspect_v, W, b):
    wq = mxq(f64(W), 1, "e4m3")
    q = l2norm((mxq(f64(aspect_v), 1, "e4m3") @ wq.T) + f64(b))
    fn = l2norm((mxq(f64(feature), 2, "e4m3") @ wq.T) + f64(b))
    return q, fn.mean(axis=1)

@@ -1,0 +1,209 @@
+from contextlib import ExitStack
+
+import concourse.mybir as mybir
+from concourse.masks import make_identity
+
+F32 = mybir.dt.float32
+BF16 = mybir.dt.bfloat16
+U32 = mybir.dt.uint32
+U8 = mybir.dt.uint8
+FP8X4 = mybir.dt.float8_e4m3fn_x4
+ALU = mybir.AluOpType
+ACT = mybir.ActivationFunctionType
+
+P = 128
+SEGMENTS = 1024
+TOKENS = 4
+K = 1024
+M = 1024
+K_PASS = 4 * P
+PASSES = K // K_PASS
+WORDS = K // 2
+BANK = 512
+HALVES = M // BANK
+GROUPS = SEGMENTS // P
+TILES_PER_GROUP = 1 + TOKENS
+ROW_TILES = GROUPS * TILES_PER_GROUP
+W_TILES = M // P
+
+AHEAD_TRANSPOSE = 3
+AHEAD_QUANTISE = 2
+GROUP_CLOSE = TILES_PER_GROUP + 1
+
+FLOPS = 2 * (SEGMENTS * TOKENS + SEGMENTS) * K * M
+
+
+def tile_linearattention_pa_kernel(tc, feature, aspect_v, W, b, out_0, out_1):
+    nc = tc.nc
+    with ExitStack() as stack:
+        const = stack.enter_context(tc.tile_pool(name="const", bufs=1))
+        raw_pool = stack.enter_context(tc.tile_pool(name="raw", bufs=GROUPS))
+        grouped_pool = stack.enter_context(tc.tile_pool(name="grouped", bufs=3))
+        mx_pool = stack.enter_context(tc.tile_pool(name="mx", bufs=4))
+        z_pool = stack.enter_context(tc.tile_pool(name="z", bufs=10))
+        scratch_pool = stack.enter_context(tc.tile_pool(name="scratch", bufs=2))
+        norm_pool = stack.enter_context(tc.tile_pool(name="norm", bufs=3))
+        out_pool = stack.enter_context(tc.tile_pool(name="out", bufs=2))
+        psum_t = stack.enter_context(tc.psum_pool(name="psum_t", bufs=2))
+        psum_y = stack.enter_context(tc.psum_pool(name="psum_y", bufs=6))
+        stack.enter_context(tc.manual_schedule())
+
+        identity = const.tile([P, P], F32)
+        make_identity(nc, identity[:])
+        norm_scale = const.tile([P, TILES_PER_GROUP], F32)
+        nc.vector.memset(norm_scale[:, 0:1], 1.0)
+        nc.vector.memset(norm_scale[:, 1:TILES_PER_GROUP], float(TOKENS * TOKENS))
+        warm = const.tile([P, 1], F32)
+        nc.vector.memset(warm[:], 1.0)
+        nc.scalar.sqrt(out=warm[:], in_=warm[:])
+
+        w_raw = const.tile([P, W_TILES * K], BF16)
+        w_raw_tiles = w_raw[:].rearrange("p (t k) -> p t k", k=K)
+        w_rows = W.rearrange("(t p) k -> p t k", p=P)
+        for t in range(0, W_TILES, 2):
+            nc.sync.dma_start(out=w_raw_tiles[:, t : t + 2, :], in_=w_rows[:, t : t + 2, :])
+        bias_bf16 = const.tile([P, M], BF16)
+        raw = {}
+        for g in range(GROUPS):
+            segments = slice(g * P, (g + 1) * P)
+            raw[g] = raw_pool.tile([P, TILES_PER_GROUP * K], BF16, name="raw")
+            nc.sync.dma_start(out=raw[g][:, 0:K], in_=aspect_v[segments, :])
+            nc.sync.dma_start(
+                out=raw[g][:, K:], in_=feature[segments, :, :].rearrange("n l d -> n (l d)")
+            )
+            if g == 0:
+                nc.sync.dma_start(out=bias_bf16[:], in_=b.partition_broadcast(P))
+
+        def transpose_rows(words, bank):
+            for j in range(WORDS // P):
+                cols = slice(j * P, (j + 1) * P)
+                nc.tensor.transpose(bank[:, cols], words[:, cols], identity[:])
+
+        def pairs_side_by_side(bank):
+            return bank.rearrange("p (c u r) -> p c r u", c=PASSES, u=2)
+
+        w_grouped = const.tile([P, PASSES * M * 4], BF16, align_bytes=64)
+        w_grouped_words = w_grouped[:].bitcast(F32).rearrange(
+            "p (c m u) -> p c m u", c=PASSES, u=2
+        )
+        w_codes = const.tile([P, PASSES * M], U32, align_bytes=64)
+        w_scales = const.tile([P, PASSES * M], U8, align_bytes=64)
+        w_words = w_raw[:].bitcast(F32)
+        for t in range(W_TILES):
+            w_bank = psum_y.tile([P, BANK], F32, name="y")
+            transpose_rows(w_words[:, t * WORDS : (t + 1) * WORDS], w_bank)
+            target = w_grouped_words[:, :, t * P : (t + 1) * P, :]
+            if t % 2 == 0:
+                nc.scalar.copy(out=target, in_=pairs_side_by_side(w_bank))
+            else:
+                nc.vector.tensor_copy(out=target, in_=pairs_side_by_side(w_bank))
+            if (t + 1) % (BANK // P) == 0:
+                h = t // (BANK // P)
+                for c in range(PASSES):
+                    lo = c * M + h * BANK
+                    nc.vector.quantize_mx(
+                        out=w_codes[:, lo : lo + BANK].bitcast(FP8X4),
+                        scales=w_scales[:, lo : lo + BANK],
+                        in_=w_grouped[:, 4 * lo : 4 * (lo + BANK)],
+                    )
+        bias = const.tile([P, M], F32)
+        nc.vector.tensor_copy(out=bias[:], in_=bias_bf16[:])
+
+        grouped = {}
+        codes = {}
+        scales = {}
+        z = {}
+        sumsq = {}
+        rnorm = {}
+        fm = {}
+
+        def transpose_and_regroup(i):
+            g, t = divmod(i, TILES_PER_GROUP)
+            x_bank = psum_t.tile([P, BANK], F32, name="xt")
+            transpose_rows(raw[g][:].bitcast(F32)[:, t * WORDS : (t + 1) * WORDS], x_bank)
+            grouped[i] = grouped_pool.tile([P, 2 * WORDS], BF16, name="grouped", align_bytes=64)
+            nc.scalar.copy(
+                out=grouped[i][:].bitcast(F32).rearrange("p (c r u) -> p c r u", c=PASSES, u=2),
+                in_=pairs_side_by_side(x_bank),
+            )
+
+        def quantise(i):
+            codes[i] = mx_pool.tile([P, PASSES * P], U32, name="codes", align_bytes=64)
+            scales[i] = mx_pool.tile([P, PASSES * P], U8, name="scales", align_bytes=64)
+            nc.vector.quantize_mx(
+                out=codes[i][:].bitcast(FP8X4), scales=scales[i][:], in_=grouped[i][:]
+            )
+
+        def multiply_and_add_bias(i):
+            z[i] = z_pool.tile([P, M], F32, name="z")
+            for h in range(HALVES):
+                y = psum_y.tile([P, BANK], F32, name="y")
+                for c in range(PASSES):
+                    rows = slice(c * P, (c + 1) * P)
+                    cols = slice(c * M + h * BANK, c * M + (h + 1) * BANK)
+                    nc.tensor.matmul_mx(
+                        out=y[:],
+                        lhsT=codes[i][:, rows].bitcast(FP8X4),
+                        lhsT_scale=scales[i][:, rows],
+                        rhs=w_codes[:, cols].bitcast(FP8X4),
+                        rhs_scale=w_scales[:, cols],
+                        start=(c == 0),
+                        stop=(c == PASSES - 1),
+                    )
+                half = slice(h * BANK, (h + 1) * BANK)
+                nc.vector.tensor_tensor(out=z[i][:, half], in0=y[:], in1=bias[:, half], op=ALU.add)
+
+        def sum_of_squares(i):
+            g, t = divmod(i, TILES_PER_GROUP)
+            if t == 0:
+                sumsq[g] = norm_pool.tile([P, TILES_PER_GROUP], F32, name="sumsq")
+            squares = scratch_pool.tile([P, M], F32, name="squares")
+            nc.scalar.activation(
+                out=squares[:], in_=z[i][:], func=ACT.Square, accum_out=sumsq[g][:, t : t + 1]
+            )
+
+        def close_group_small(g, phase):
+            if phase == 0:
+                clamped = norm_pool.tile([P, TILES_PER_GROUP], F32, name="clamped")
+                nc.vector.scalar_tensor_tensor(
+                    out=clamped[:], in0=sumsq[g][:], scalar=1e-24, in1=norm_scale[:],
+                    op0=ALU.max, op1=ALU.mult,
+                )
+                rnorm[g] = norm_pool.tile([P, TILES_PER_GROUP], F32, name="rnorm")
+                nc.scalar.sqrt(out=rnorm[g][:], in_=clamped[:])
+            if phase == 1:
+                nc.vector.reciprocal(out=rnorm[g][:], in_=rnorm[g][:])
+
+        def close_group_big(g, phase):
+            first = g * TILES_PER_GROUP
+            segments = slice(g * P, (g + 1) * P)
+            if phase == 1:
+                q = out_pool.tile([P, M], F32, name="q")
+                nc.scalar.activation(out=q[:], in_=z[first][:], func=ACT.Copy, scale=rnorm[g][:, 0:1])
+                nc.sync.dma_start(out=out_0[segments, :], in_=q[:])
+                fm[g] = out_pool.tile([P, M], F32, name="fm")
+                nc.scalar.activation(
+                    out=fm[g][:], in_=z[first + 1][:], func=ACT.Copy, scale=rnorm[g][:, 1:2]
+                )
+            if phase >= 2:
+                nc.vector.scalar_tensor_tensor(
+                    out=fm[g][:], in0=z[first + phase][:], scalar=rnorm[g][:, phase : phase + 1],
+                    in1=fm[g][:], op0=ALU.mult, op1=ALU.add,
+                )
+            if phase == TILES_PER_GROUP - 1:
+                nc.sync.dma_start(out=out_1[segments, :], in_=fm[g][:])
+
+        for step in range(-AHEAD_TRANSPOSE, ROW_TILES + GROUP_CLOSE):
+            closing, phase = divmod(step - GROUP_CLOSE, TILES_PER_GROUP)
+            if closing >= 0:
+                close_group_small(closing, phase)
+            if step + AHEAD_TRANSPOSE < ROW_TILES:
+                transpose_and_regroup(step + AHEAD_TRANSPOSE)
+            if 0 <= step + AHEAD_QUANTISE < ROW_TILES:
+                quantise(step + AHEAD_QUANTISE)
+            if 0 <= step < ROW_TILES:
+                multiply_and_add_bias(step)
+            if 0 <= step - 1 < ROW_TILES:
+                sum_of_squares(step - 1)
+            if closing >= 0:
+                close_group_big(closing, phase)

@@ -28,7 +28,8 @@ W_TILES = M // P
 
 AHEAD_TRANSPOSE = 3
 AHEAD_QUANTISE = 2
-GROUP_CLOSE = TILES_PER_GROUP + 1
+BEHIND_NORM = 1
+BEHIND_MEAN = 3
 
 FLOPS = 2 * (SEGMENTS * TOKENS + SEGMENTS) * K * M
 
@@ -40,9 +41,9 @@ def tile_linearattention_pa_kernel(tc, feature, aspect_v, W, b, out_0, out_1):
         raw_pool = stack.enter_context(tc.tile_pool(name="raw", bufs=GROUPS))
         grouped_pool = stack.enter_context(tc.tile_pool(name="grouped", bufs=3))
         mx_pool = stack.enter_context(tc.tile_pool(name="mx", bufs=4))
-        z_pool = stack.enter_context(tc.tile_pool(name="z", bufs=10))
+        z_pool = stack.enter_context(tc.tile_pool(name="z", bufs=6))
         scratch_pool = stack.enter_context(tc.tile_pool(name="scratch", bufs=2))
-        norm_pool = stack.enter_context(tc.tile_pool(name="norm", bufs=3))
+        norm_pool = stack.enter_context(tc.tile_pool(name="norm", bufs=8))
         out_pool = stack.enter_context(tc.tile_pool(name="out", bufs=2))
         psum_t = stack.enter_context(tc.psum_pool(name="psum_t", bufs=2))
         psum_y = stack.enter_context(tc.psum_pool(name="psum_y", bufs=6))
@@ -50,19 +51,19 @@ def tile_linearattention_pa_kernel(tc, feature, aspect_v, W, b, out_0, out_1):
 
         identity = const.tile([P, P], F32)
         make_identity(nc, identity[:])
-        norm_scale = const.tile([P, TILES_PER_GROUP], F32)
-        nc.vector.memset(norm_scale[:, 0:1], 1.0)
-        nc.vector.memset(norm_scale[:, 1:TILES_PER_GROUP], float(TOKENS * TOKENS))
-        warm = const.tile([P, 1], F32)
-        nc.vector.memset(warm[:], 1.0)
-        nc.scalar.sqrt(out=warm[:], in_=warm[:])
+        minus_half = const.tile([P, 1], F32)
+        nc.vector.memset(minus_half[:], -0.5)
+        ones = const.tile([P, P], BF16)
+        nc.vector.memset(ones[:], 1.0)
+        bias_row = const.tile([P, M], BF16)
+        nc.vector.memset(bias_row[:], 0.0)
+        nc.scalar.dma_start(out=bias_row[0:1, :], in_=b.rearrange("(o m) -> o m", o=1))
 
         w_raw = const.tile([P, W_TILES * K], BF16)
         w_raw_tiles = w_raw[:].rearrange("p (t k) -> p t k", k=K)
         w_rows = W.rearrange("(t p) k -> p t k", p=P)
         for t in range(0, W_TILES, 2):
             nc.sync.dma_start(out=w_raw_tiles[:, t : t + 2, :], in_=w_rows[:, t : t + 2, :])
-        bias_bf16 = const.tile([P, M], BF16)
         raw = {}
         for g in range(GROUPS):
             segments = slice(g * P, (g + 1) * P)
@@ -71,8 +72,6 @@ def tile_linearattention_pa_kernel(tc, feature, aspect_v, W, b, out_0, out_1):
             nc.sync.dma_start(
                 out=raw[g][:, K:], in_=feature[segments, :, :].rearrange("n l d -> n (l d)")
             )
-            if g == 0:
-                nc.sync.dma_start(out=bias_bf16[:], in_=b.partition_broadcast(P))
 
         def transpose_rows(words, bank):
             for j in range(WORDS // P):
@@ -81,6 +80,13 @@ def tile_linearattention_pa_kernel(tc, feature, aspect_v, W, b, out_0, out_1):
 
         def pairs_side_by_side(bank):
             return bank.rearrange("p (c u r) -> p c r u", c=PASSES, u=2)
+
+        bias = const.tile([P, M], F32)
+        for h in range(HALVES):
+            half = slice(h * BANK, (h + 1) * BANK)
+            b_bank = psum_y.tile([P, BANK], F32, name="y")
+            nc.tensor.matmul(out=b_bank[:], lhsT=ones[:], rhs=bias_row[:, half], start=True, stop=True)
+            nc.scalar.copy(out=bias[:, half], in_=b_bank[:])
 
         w_grouped = const.tile([P, PASSES * M * 4], BF16, align_bytes=64)
         w_grouped_words = w_grouped[:].bitcast(F32).rearrange(
@@ -106,8 +112,6 @@ def tile_linearattention_pa_kernel(tc, feature, aspect_v, W, b, out_0, out_1):
                         scales=w_scales[:, lo : lo + BANK],
                         in_=w_grouped[:, 4 * lo : 4 * (lo + BANK)],
                     )
-        bias = const.tile([P, M], F32)
-        nc.vector.tensor_copy(out=bias[:], in_=bias_bf16[:])
 
         grouped = {}
         codes = {}
@@ -154,56 +158,50 @@ def tile_linearattention_pa_kernel(tc, feature, aspect_v, W, b, out_0, out_1):
                 nc.vector.tensor_tensor(out=z[i][:, half], in0=y[:], in1=bias[:, half], op=ALU.add)
 
         def sum_of_squares(i):
-            g, t = divmod(i, TILES_PER_GROUP)
-            if t == 0:
-                sumsq[g] = norm_pool.tile([P, TILES_PER_GROUP], F32, name="sumsq")
+            sumsq[i] = norm_pool.tile([P, 1], F32, name="sumsq")
             squares = scratch_pool.tile([P, M], F32, name="squares")
-            nc.scalar.activation(
-                out=squares[:], in_=z[i][:], func=ACT.Square, accum_out=sumsq[g][:, t : t + 1]
+            nc.scalar.activation(out=squares[:], in_=z[i][:], func=ACT.Square, accum_out=sumsq[i][:])
+
+        def reciprocal_norm(i):
+            g, t = divmod(i, TILES_PER_GROUP)
+            clamped = norm_pool.tile([P, 1], F32, name="clamped")
+            nc.gpsimd.tensor_scalar(
+                out=clamped[:], in0=sumsq[i][:], scalar1=1e-24,
+                scalar2=(1.0 if t == 0 else float(TOKENS * TOKENS)), op0=ALU.max, op1=ALU.mult,
             )
-
-        def close_group_small(g, phase):
-            if phase == 0:
-                clamped = norm_pool.tile([P, TILES_PER_GROUP], F32, name="clamped")
-                nc.vector.scalar_tensor_tensor(
-                    out=clamped[:], in0=sumsq[g][:], scalar=1e-24, in1=norm_scale[:],
-                    op0=ALU.max, op1=ALU.mult,
-                )
-                rnorm[g] = norm_pool.tile([P, TILES_PER_GROUP], F32, name="rnorm")
-                nc.scalar.sqrt(out=rnorm[g][:], in_=clamped[:])
-            if phase == 1:
-                nc.vector.reciprocal(out=rnorm[g][:], in_=rnorm[g][:])
-
-        def close_group_big(g, phase):
-            first = g * TILES_PER_GROUP
-            segments = slice(g * P, (g + 1) * P)
-            if phase == 1:
+            rnorm[i] = norm_pool.tile([P, 1], F32, name="rnorm")
+            nc.gpsimd.tensor_tensor(out=rnorm[i][:], in0=clamped[:], in1=minus_half[:], op=ALU.pow)
+            if t == 0:
                 q = out_pool.tile([P, M], F32, name="q")
-                nc.scalar.activation(out=q[:], in_=z[first][:], func=ACT.Copy, scale=rnorm[g][:, 0:1])
-                nc.sync.dma_start(out=out_0[segments, :], in_=q[:])
+                nc.gpsimd.tensor_scalar(
+                    out=q[:], in0=z[i][:], scalar1=rnorm[i][:], scalar2=0.0, op0=ALU.mult, op1=ALU.add
+                )
+                nc.sync.dma_start(out=out_0[g * P : (g + 1) * P, :], in_=q[:])
+            if t == 1:
                 fm[g] = out_pool.tile([P, M], F32, name="fm")
-                nc.scalar.activation(
-                    out=fm[g][:], in_=z[first + 1][:], func=ACT.Copy, scale=rnorm[g][:, 1:2]
+                nc.gpsimd.tensor_scalar(
+                    out=fm[g][:], in0=z[i][:], scalar1=rnorm[i][:], scalar2=0.0, op0=ALU.mult, op1=ALU.add
                 )
-            if phase >= 2:
-                nc.vector.scalar_tensor_tensor(
-                    out=fm[g][:], in0=z[first + phase][:], scalar=rnorm[g][:, phase : phase + 1],
-                    in1=fm[g][:], op0=ALU.mult, op1=ALU.add,
-                )
-            if phase == TILES_PER_GROUP - 1:
-                nc.sync.dma_start(out=out_1[segments, :], in_=fm[g][:])
 
-        for step in range(-AHEAD_TRANSPOSE, ROW_TILES + GROUP_CLOSE):
-            closing, phase = divmod(step - GROUP_CLOSE, TILES_PER_GROUP)
-            if closing >= 0:
-                close_group_small(closing, phase)
+        def add_to_mean(i):
+            g, t = divmod(i, TILES_PER_GROUP)
+            if t >= 2:
+                nc.vector.scalar_tensor_tensor(
+                    out=fm[g][:], in0=z[i][:], scalar=rnorm[i][:], in1=fm[g][:],
+                    op0=ALU.mult, op1=ALU.add,
+                )
+            if t == TILES_PER_GROUP - 1:
+                nc.sync.dma_start(out=out_1[g * P : (g + 1) * P, :], in_=fm[g][:])
+
+        for step in range(-AHEAD_TRANSPOSE, ROW_TILES + BEHIND_MEAN):
             if step + AHEAD_TRANSPOSE < ROW_TILES:
                 transpose_and_regroup(step + AHEAD_TRANSPOSE)
             if 0 <= step + AHEAD_QUANTISE < ROW_TILES:
                 quantise(step + AHEAD_QUANTISE)
             if 0 <= step < ROW_TILES:
                 multiply_and_add_bias(step)
-            if 0 <= step - 1 < ROW_TILES:
-                sum_of_squares(step - 1)
-            if closing >= 0:
-                close_group_big(closing, phase)
+            if 0 <= step - BEHIND_NORM < ROW_TILES:
+                sum_of_squares(step - BEHIND_NORM)
+                reciprocal_norm(step - BEHIND_NORM)
+            if 0 <= step - BEHIND_MEAN < ROW_TILES:
+                add_to_mean(step - BEHIND_MEAN)

@@ -26,10 +26,11 @@ TILES_PER_GROUP = 1 + TOKENS
 ROW_TILES = GROUPS * TILES_PER_GROUP
 W_TILES = M // P
 
-AHEAD_TRANSPOSE = 3
+AHEAD_TRANSPOSE = 4
 AHEAD_QUANTISE = 2
-BEHIND_NORM = 1
-BEHIND_MEAN = 3
+BEHIND_NORM = 2
+BEHIND_SCALE = 4
+BEHIND_MEAN = 6
 
 FLOPS = 2 * (SEGMENTS * TOKENS + SEGMENTS) * K * M
 
@@ -39,11 +40,11 @@ def tile_linearattention_pa_kernel(tc, feature, aspect_v, W, b, out_0, out_1):
     with ExitStack() as stack:
         const = stack.enter_context(tc.tile_pool(name="const", bufs=1))
         raw_pool = stack.enter_context(tc.tile_pool(name="raw", bufs=GROUPS))
-        grouped_pool = stack.enter_context(tc.tile_pool(name="grouped", bufs=3))
+        grouped_pool = stack.enter_context(tc.tile_pool(name="grouped", bufs=4))
         mx_pool = stack.enter_context(tc.tile_pool(name="mx", bufs=4))
-        z_pool = stack.enter_context(tc.tile_pool(name="z", bufs=6))
+        z_pool = stack.enter_context(tc.tile_pool(name="z", bufs=9))
         scratch_pool = stack.enter_context(tc.tile_pool(name="scratch", bufs=2))
-        norm_pool = stack.enter_context(tc.tile_pool(name="norm", bufs=8))
+        norm_pool = stack.enter_context(tc.tile_pool(name="norm", bufs=9))
         out_pool = stack.enter_context(tc.tile_pool(name="out", bufs=2))
         psum_t = stack.enter_context(tc.psum_pool(name="psum_t", bufs=2))
         psum_y = stack.enter_context(tc.psum_pool(name="psum_y", bufs=6))
@@ -57,8 +58,8 @@ def tile_linearattention_pa_kernel(tc, feature, aspect_v, W, b, out_0, out_1):
         nc.vector.memset(ones[:], 1.0)
         bias_row = const.tile([P, M], BF16)
         nc.vector.memset(bias_row[:], 0.0)
-        nc.scalar.dma_start(out=bias_row[0:1, :], in_=b.rearrange("(o m) -> o m", o=1))
 
+        nc.sync.dma_start(out=bias_row[0:1, :], in_=b.rearrange("(o m) -> o m", o=1))
         w_raw = const.tile([P, W_TILES * K], BF16)
         w_raw_tiles = w_raw[:].rearrange("p (t k) -> p t k", k=K)
         w_rows = W.rearrange("(t p) k -> p t k", p=P)
@@ -69,9 +70,8 @@ def tile_linearattention_pa_kernel(tc, feature, aspect_v, W, b, out_0, out_1):
             segments = slice(g * P, (g + 1) * P)
             raw[g] = raw_pool.tile([P, TILES_PER_GROUP * K], BF16, name="raw")
             nc.sync.dma_start(out=raw[g][:, 0:K], in_=aspect_v[segments, :])
-            nc.sync.dma_start(
-                out=raw[g][:, K:], in_=feature[segments, :, :].rearrange("n l d -> n (l d)")
-            )
+            for l in range(TOKENS):
+                nc.sync.dma_start(out=raw[g][:, (1 + l) * K : (2 + l) * K], in_=feature[segments, l, :])
 
         def transpose_rows(words, bank):
             for j in range(WORDS // P):
@@ -80,13 +80,6 @@ def tile_linearattention_pa_kernel(tc, feature, aspect_v, W, b, out_0, out_1):
 
         def pairs_side_by_side(bank):
             return bank.rearrange("p (c u r) -> p c r u", c=PASSES, u=2)
-
-        bias = const.tile([P, M], F32)
-        for h in range(HALVES):
-            half = slice(h * BANK, (h + 1) * BANK)
-            b_bank = psum_y.tile([P, BANK], F32, name="y")
-            nc.tensor.matmul(out=b_bank[:], lhsT=ones[:], rhs=bias_row[:, half], start=True, stop=True)
-            nc.scalar.copy(out=bias[:, half], in_=b_bank[:])
 
         w_grouped = const.tile([P, PASSES * M * 4], BF16, align_bytes=64)
         w_grouped_words = w_grouped[:].bitcast(F32).rearrange(
@@ -112,6 +105,13 @@ def tile_linearattention_pa_kernel(tc, feature, aspect_v, W, b, out_0, out_1):
                         scales=w_scales[:, lo : lo + BANK],
                         in_=w_grouped[:, 4 * lo : 4 * (lo + BANK)],
                     )
+
+        bias = const.tile([P, M], F32)
+        for h in range(HALVES):
+            half = slice(h * BANK, (h + 1) * BANK)
+            b_bank = psum_y.tile([P, BANK], F32, name="y")
+            nc.tensor.matmul(out=b_bank[:], lhsT=ones[:], rhs=bias_row[:, half], start=True, stop=True)
+            nc.scalar.copy(out=bias[:, half], in_=b_bank[:])
 
         grouped = {}
         codes = {}
@@ -163,7 +163,7 @@ def tile_linearattention_pa_kernel(tc, feature, aspect_v, W, b, out_0, out_1):
             nc.scalar.activation(out=squares[:], in_=z[i][:], func=ACT.Square, accum_out=sumsq[i][:])
 
         def reciprocal_norm(i):
-            g, t = divmod(i, TILES_PER_GROUP)
+            t = i % TILES_PER_GROUP
             clamped = norm_pool.tile([P, 1], F32, name="clamped")
             nc.gpsimd.tensor_scalar(
                 out=clamped[:], in0=sumsq[i][:], scalar1=1e-24,
@@ -171,17 +171,16 @@ def tile_linearattention_pa_kernel(tc, feature, aspect_v, W, b, out_0, out_1):
             )
             rnorm[i] = norm_pool.tile([P, 1], F32, name="rnorm")
             nc.gpsimd.tensor_tensor(out=rnorm[i][:], in0=clamped[:], in1=minus_half[:], op=ALU.pow)
+
+        def scale(i):
+            g, t = divmod(i, TILES_PER_GROUP)
             if t == 0:
                 q = out_pool.tile([P, M], F32, name="q")
-                nc.gpsimd.tensor_scalar(
-                    out=q[:], in0=z[i][:], scalar1=rnorm[i][:], scalar2=0.0, op0=ALU.mult, op1=ALU.add
-                )
+                nc.scalar.activation(out=q[:], in_=z[i][:], func=ACT.Copy, scale=rnorm[i][:])
                 nc.sync.dma_start(out=out_0[g * P : (g + 1) * P, :], in_=q[:])
             if t == 1:
                 fm[g] = out_pool.tile([P, M], F32, name="fm")
-                nc.gpsimd.tensor_scalar(
-                    out=fm[g][:], in0=z[i][:], scalar1=rnorm[i][:], scalar2=0.0, op0=ALU.mult, op1=ALU.add
-                )
+                nc.scalar.activation(out=fm[g][:], in_=z[i][:], func=ACT.Copy, scale=rnorm[i][:])
 
         def add_to_mean(i):
             g, t = divmod(i, TILES_PER_GROUP)
@@ -194,14 +193,16 @@ def tile_linearattention_pa_kernel(tc, feature, aspect_v, W, b, out_0, out_1):
                 nc.sync.dma_start(out=out_1[g * P : (g + 1) * P, :], in_=fm[g][:])
 
         for step in range(-AHEAD_TRANSPOSE, ROW_TILES + BEHIND_MEAN):
+            if 0 <= step < ROW_TILES:
+                multiply_and_add_bias(step)
             if step + AHEAD_TRANSPOSE < ROW_TILES:
                 transpose_and_regroup(step + AHEAD_TRANSPOSE)
             if 0 <= step + AHEAD_QUANTISE < ROW_TILES:
                 quantise(step + AHEAD_QUANTISE)
-            if 0 <= step < ROW_TILES:
-                multiply_and_add_bias(step)
             if 0 <= step - BEHIND_NORM < ROW_TILES:
                 sum_of_squares(step - BEHIND_NORM)
                 reciprocal_norm(step - BEHIND_NORM)
+            if 0 <= step - BEHIND_SCALE < ROW_TILES:
+                scale(step - BEHIND_SCALE)
             if 0 <= step - BEHIND_MEAN < ROW_TILES:
                 add_to_mean(step - BEHIND_MEAN)

@@ -28,9 +28,9 @@ W_TILES = M // P
 
 AHEAD_TRANSPOSE = 4
 AHEAD_QUANTISE = 2
-BEHIND_NORM = 2
-BEHIND_SCALE = 4
-BEHIND_MEAN = 6
+BEHIND_NORM = 1
+BEHIND_SCALE = 3
+BEHIND_MEAN = 4
 
 FLOPS = 2 * (SEGMENTS * TOKENS + SEGMENTS) * K * M
 
@@ -48,30 +48,40 @@ def tile_linearattention_pa_kernel(tc, feature, aspect_v, W, b, out_0, out_1):
         out_pool = stack.enter_context(tc.tile_pool(name="out", bufs=2))
         psum_t = stack.enter_context(tc.psum_pool(name="psum_t", bufs=2))
         psum_y = stack.enter_context(tc.psum_pool(name="psum_y", bufs=6))
-        stack.enter_context(tc.manual_schedule())
 
-        identity = const.tile([P, P], F32)
-        make_identity(nc, identity[:])
-        minus_half = const.tile([P, 1], F32)
-        nc.vector.memset(minus_half[:], -0.5)
-        ones = const.tile([P, P], BF16)
-        nc.vector.memset(ones[:], 1.0)
         bias_row = const.tile([P, M], BF16)
         nc.vector.memset(bias_row[:], 0.0)
+        ones = const.tile([P, P], BF16)
+        nc.vector.memset(ones[:], 1.0)
+        minus_half = const.tile([P, 1], F32)
+        nc.vector.memset(minus_half[:], -0.5)
+        identity = const.tile([P, P], F32)
+        make_identity(nc, identity[:])
 
-        nc.sync.dma_start(out=bias_row[0:1, :], in_=b.rearrange("(o m) -> o m", o=1))
         w_raw = const.tile([P, W_TILES * K], BF16)
         w_raw_tiles = w_raw[:].rearrange("p (t k) -> p t k", k=K)
         w_rows = W.rearrange("(t p) k -> p t k", p=P)
-        for t in range(0, W_TILES, 2):
-            nc.sync.dma_start(out=w_raw_tiles[:, t : t + 2, :], in_=w_rows[:, t : t + 2, :])
         raw = {}
         for g in range(GROUPS):
-            segments = slice(g * P, (g + 1) * P)
             raw[g] = raw_pool.tile([P, TILES_PER_GROUP * K], BF16, name="raw")
-            nc.sync.dma_start(out=raw[g][:, 0:K], in_=aspect_v[segments, :])
-            for l in range(TOKENS):
-                nc.sync.dma_start(out=raw[g][:, (1 + l) * K : (2 + l) * K], in_=feature[segments, l, :])
+
+        def load_w(t):
+            nc.sync.dma_start(out=w_raw_tiles[:, t : t + 2, :], in_=w_rows[:, t : t + 2, :])
+
+        def load_rows(i):
+            g, t = divmod(i, TILES_PER_GROUP)
+            segments = slice(g * P, (g + 1) * P)
+            rows = aspect_v[segments, :] if t == 0 else feature[segments, t - 1, :]
+            nc.sync.dma_start(out=raw[g][:, t * K : (t + 1) * K], in_=rows)
+
+        load_w(0)
+        nc.sync.dma_start(out=bias_row[0:1, :], in_=b.rearrange("(o m) -> o m", o=1))
+        load_w(2)
+        load_rows(0)
+        load_w(4)
+        load_w(6)
+        for i in range(1, ROW_TILES):
+            load_rows(i)
 
         def transpose_rows(words, bank):
             for j in range(WORDS // P):
@@ -80,6 +90,13 @@ def tile_linearattention_pa_kernel(tc, feature, aspect_v, W, b, out_0, out_1):
 
         def pairs_side_by_side(bank):
             return bank.rearrange("p (c u r) -> p c r u", c=PASSES, u=2)
+
+        bias = const.tile([P, M], F32)
+        for h in range(HALVES):
+            half = slice(h * BANK, (h + 1) * BANK)
+            b_bank = psum_y.tile([P, BANK], F32, name="y")
+            nc.tensor.matmul(out=b_bank[:], lhsT=ones[:], rhs=bias_row[:, half], start=True, stop=True)
+            nc.vector.tensor_copy(out=bias[:, half], in_=b_bank[:])
 
         w_grouped = const.tile([P, PASSES * M * 4], BF16, align_bytes=64)
         w_grouped_words = w_grouped[:].bitcast(F32).rearrange(
@@ -105,13 +122,6 @@ def tile_linearattention_pa_kernel(tc, feature, aspect_v, W, b, out_0, out_1):
                         scales=w_scales[:, lo : lo + BANK],
                         in_=w_grouped[:, 4 * lo : 4 * (lo + BANK)],
                     )
-
-        bias = const.tile([P, M], F32)
-        for h in range(HALVES):
-            half = slice(h * BANK, (h + 1) * BANK)
-            b_bank = psum_y.tile([P, BANK], F32, name="y")
-            nc.tensor.matmul(out=b_bank[:], lhsT=ones[:], rhs=bias_row[:, half], start=True, stop=True)
-            nc.scalar.copy(out=bias[:, half], in_=b_bank[:])
 
         grouped = {}
         codes = {}

@@ -25,12 +25,22 @@ GROUPS = SEGMENTS // P
 TILES_PER_GROUP = 1 + TOKENS
 ROW_TILES = GROUPS * TILES_PER_GROUP
 W_TILES = M // P
+W_TILES_PER_HALF = BANK // P
+W_TILES_PER_LOAD = 2
 
 AHEAD_TRANSPOSE = 4
 AHEAD_QUANTISE = 2
-BEHIND_NORM = 1
-BEHIND_SCALE = 3
-BEHIND_MEAN = 4
+BEHIND_NORM = 2
+BEHIND_SCALE = 4
+BEHIND_MEAN = 6
+
+GROUPED_BUFS = 4
+MX_BUFS = 4
+Z_BUFS = 9
+SQUARES_BUFS = 2
+OUT_BUFS = 2
+TRANSPOSE_BANKS = 2
+PRODUCT_BANKS = 6
 
 FLOPS = 2 * (SEGMENTS * TOKENS + SEGMENTS) * K * M
 
@@ -40,14 +50,14 @@ def tile_linearattention_pa_kernel(tc, feature, aspect_v, W, b, out_0, out_1):
     with ExitStack() as stack:
         const = stack.enter_context(tc.tile_pool(name="const", bufs=1))
         raw_pool = stack.enter_context(tc.tile_pool(name="raw", bufs=GROUPS))
-        grouped_pool = stack.enter_context(tc.tile_pool(name="grouped", bufs=4))
-        mx_pool = stack.enter_context(tc.tile_pool(name="mx", bufs=4))
-        z_pool = stack.enter_context(tc.tile_pool(name="z", bufs=9))
-        scratch_pool = stack.enter_context(tc.tile_pool(name="scratch", bufs=2))
-        norm_pool = stack.enter_context(tc.tile_pool(name="norm", bufs=9))
-        out_pool = stack.enter_context(tc.tile_pool(name="out", bufs=2))
-        psum_t = stack.enter_context(tc.psum_pool(name="psum_t", bufs=2))
-        psum_y = stack.enter_context(tc.psum_pool(name="psum_y", bufs=6))
+        grouped_pool = stack.enter_context(tc.tile_pool(name="grouped", bufs=GROUPED_BUFS))
+        mx_pool = stack.enter_context(tc.tile_pool(name="mx", bufs=MX_BUFS))
+        z_pool = stack.enter_context(tc.tile_pool(name="z", bufs=Z_BUFS))
+        scratch_pool = stack.enter_context(tc.tile_pool(name="scratch", bufs=SQUARES_BUFS))
+        norm_pool = stack.enter_context(tc.tile_pool(name="norm", bufs=Z_BUFS))
+        out_pool = stack.enter_context(tc.tile_pool(name="out", bufs=OUT_BUFS))
+        psum_t = stack.enter_context(tc.psum_pool(name="psum_t", bufs=TRANSPOSE_BANKS))
+        psum_y = stack.enter_context(tc.psum_pool(name="psum_y", bufs=PRODUCT_BANKS))
 
         bias_row = const.tile([P, M], BF16)
         nc.vector.memset(bias_row[:], 0.0)
@@ -65,21 +75,22 @@ def tile_linearattention_pa_kernel(tc, feature, aspect_v, W, b, out_0, out_1):
         for g in range(GROUPS):
             raw[g] = raw_pool.tile([P, TILES_PER_GROUP * K], BF16, name="raw")
 
-        def load_w(t):
-            nc.sync.dma_start(out=w_raw_tiles[:, t : t + 2, :], in_=w_rows[:, t : t + 2, :])
+        def load_w(first):
+            tiles = slice(first, first + W_TILES_PER_LOAD)
+            nc.sync.dma_start(out=w_raw_tiles[:, tiles, :], in_=w_rows[:, tiles, :])
 
         def load_rows(i):
             g, t = divmod(i, TILES_PER_GROUP)
             segments = slice(g * P, (g + 1) * P)
-            rows = aspect_v[segments, :] if t == 0 else feature[segments, t - 1, :]
-            nc.sync.dma_start(out=raw[g][:, t * K : (t + 1) * K], in_=rows)
+            source = aspect_v[segments, :] if t == 0 else feature[segments, t - 1, :]
+            nc.sync.dma_start(out=raw[g][:, t * K : (t + 1) * K], in_=source)
 
         load_w(0)
         nc.sync.dma_start(out=bias_row[0:1, :], in_=b.rearrange("(o m) -> o m", o=1))
-        load_w(2)
+        load_w(W_TILES_PER_LOAD)
         load_rows(0)
-        load_w(4)
-        load_w(6)
+        for first in range(W_TILES_PER_HALF, W_TILES, W_TILES_PER_LOAD):
+            load_w(first)
         for i in range(1, ROW_TILES):
             load_rows(i)
 
@@ -105,16 +116,16 @@ def tile_linearattention_pa_kernel(tc, feature, aspect_v, W, b, out_0, out_1):
         w_codes = const.tile([P, PASSES * M], U32, align_bytes=64)
         w_scales = const.tile([P, PASSES * M], U8, align_bytes=64)
         w_words = w_raw[:].bitcast(F32)
-        for t in range(W_TILES):
+        for wt in range(W_TILES):
             w_bank = psum_y.tile([P, BANK], F32, name="y")
-            transpose_rows(w_words[:, t * WORDS : (t + 1) * WORDS], w_bank)
-            target = w_grouped_words[:, :, t * P : (t + 1) * P, :]
-            if t % 2 == 0:
+            transpose_rows(w_words[:, wt * WORDS : (wt + 1) * WORDS], w_bank)
+            target = w_grouped_words[:, :, wt * P : (wt + 1) * P, :]
+            if wt % 2 == 0:
                 nc.scalar.copy(out=target, in_=pairs_side_by_side(w_bank))
             else:
                 nc.vector.tensor_copy(out=target, in_=pairs_side_by_side(w_bank))
-            if (t + 1) % (BANK // P) == 0:
-                h = t // (BANK // P)
+            if (wt + 1) % W_TILES_PER_HALF == 0:
+                h = wt // W_TILES_PER_HALF
                 for c in range(PASSES):
                     lo = c * M + h * BANK
                     nc.vector.quantize_mx(
@@ -153,14 +164,14 @@ def tile_linearattention_pa_kernel(tc, feature, aspect_v, W, b, out_0, out_1):
             for h in range(HALVES):
                 y = psum_y.tile([P, BANK], F32, name="y")
                 for c in range(PASSES):
-                    rows = slice(c * P, (c + 1) * P)
-                    cols = slice(c * M + h * BANK, c * M + (h + 1) * BANK)
+                    x_cols = slice(c * P, (c + 1) * P)
+                    w_cols = slice(c * M + h * BANK, c * M + (h + 1) * BANK)
                     nc.tensor.matmul_mx(
                         out=y[:],
-                        lhsT=codes[i][:, rows].bitcast(FP8X4),
-                        lhsT_scale=scales[i][:, rows],
-                        rhs=w_codes[:, cols].bitcast(FP8X4),
-                        rhs_scale=w_scales[:, cols],
+                        lhsT=codes[i][:, x_cols].bitcast(FP8X4),
+                        lhsT_scale=scales[i][:, x_cols],
+                        rhs=w_codes[:, w_cols].bitcast(FP8X4),
+                        rhs_scale=w_scales[:, w_cols],
                         start=(c == 0),
                         stop=(c == PASSES - 1),
                     )
@@ -182,7 +193,7 @@ def tile_linearattention_pa_kernel(tc, feature, aspect_v, W, b, out_0, out_1):
             rnorm[i] = norm_pool.tile([P, 1], F32, name="rnorm")
             nc.gpsimd.tensor_tensor(out=rnorm[i][:], in0=clamped[:], in1=minus_half[:], op=ALU.pow)
 
-        def scale(i):
+        def normalise_alone(i):
             g, t = divmod(i, TILES_PER_GROUP)
             if t == 0:
                 q = out_pool.tile([P, M], F32, name="q")
@@ -213,6 +224,6 @@ def tile_linearattention_pa_kernel(tc, feature, aspect_v, W, b, out_0, out_1):
                 sum_of_squares(step - BEHIND_NORM)
                 reciprocal_norm(step - BEHIND_NORM)
             if 0 <= step - BEHIND_SCALE < ROW_TILES:
-                scale(step - BEHIND_SCALE)
+                normalise_alone(step - BEHIND_SCALE)
             if 0 <= step - BEHIND_MEAN < ROW_TILES:
                 add_to_mean(step - BEHIND_MEAN)

from contextlib import ExitStack

import concourse.mybir as mybir
from concourse.masks import make_identity

F32 = mybir.dt.float32
BF16 = mybir.dt.bfloat16
U32 = mybir.dt.uint32
U8 = mybir.dt.uint8
FP8X4 = mybir.dt.float8_e4m3fn_x4
ALU = mybir.AluOpType
ACT = mybir.ActivationFunctionType

P = 128
SEGMENTS = 1024
TOKENS = 4
K = 1024
M = 1024
K_PASS = 4 * P
PASSES = K // K_PASS
WORDS = K // 2
BANK = 512
HALVES = M // BANK
GROUPS = SEGMENTS // P
TILES_PER_GROUP = 1 + TOKENS
ROW_TILES = GROUPS * TILES_PER_GROUP
W_TILES = M // P
W_TILES_PER_HALF = BANK // P
W_TILES_PER_LOAD = 2

AHEAD_TRANSPOSE = 4
AHEAD_QUANTISE = 2
BEHIND_NORM = 2
BEHIND_SCALE = 4
BEHIND_MEAN = 6

GROUPED_BUFS = 4
MX_BUFS = 4
Z_BUFS = 9
SQUARES_BUFS = 2
OUT_BUFS = 2
TRANSPOSE_BANKS = 2
PRODUCT_BANKS = 6

FLOPS = 2 * (SEGMENTS * TOKENS + SEGMENTS) * K * M


def tile_linearattention_pa_kernel(tc, feature, aspect_v, W, b, out_0, out_1):
    nc = tc.nc
    with ExitStack() as stack:
        const = stack.enter_context(tc.tile_pool(name="const", bufs=1))
        raw_pool = stack.enter_context(tc.tile_pool(name="raw", bufs=GROUPS))
        grouped_pool = stack.enter_context(tc.tile_pool(name="grouped", bufs=GROUPED_BUFS))
        mx_pool = stack.enter_context(tc.tile_pool(name="mx", bufs=MX_BUFS))
        z_pool = stack.enter_context(tc.tile_pool(name="z", bufs=Z_BUFS))
        scratch_pool = stack.enter_context(tc.tile_pool(name="scratch", bufs=SQUARES_BUFS))
        norm_pool = stack.enter_context(tc.tile_pool(name="norm", bufs=Z_BUFS))
        out_pool = stack.enter_context(tc.tile_pool(name="out", bufs=OUT_BUFS))
        psum_t = stack.enter_context(tc.psum_pool(name="psum_t", bufs=TRANSPOSE_BANKS))
        psum_y = stack.enter_context(tc.psum_pool(name="psum_y", bufs=PRODUCT_BANKS))

        bias_row = const.tile([P, M], BF16)
        nc.vector.memset(bias_row[:], 0.0)
        ones = const.tile([P, P], BF16)
        nc.vector.memset(ones[:], 1.0)
        minus_half = const.tile([P, 1], F32)
        nc.vector.memset(minus_half[:], -0.5)
        identity = const.tile([P, P], F32)
        make_identity(nc, identity[:])

        w_raw = const.tile([P, W_TILES * K], BF16)
        w_raw_tiles = w_raw[:].rearrange("p (t k) -> p t k", k=K)
        w_rows = W.rearrange("(t p) k -> p t k", p=P)
        raw = {}
        for g in range(GROUPS):
            raw[g] = raw_pool.tile([P, TILES_PER_GROUP * K], BF16, name="raw")

        def load_w(first):
            tiles = slice(first, first + W_TILES_PER_LOAD)
            nc.sync.dma_start(out=w_raw_tiles[:, tiles, :], in_=w_rows[:, tiles, :])

        def load_rows(i):
            g, t = divmod(i, TILES_PER_GROUP)
            segments = slice(g * P, (g + 1) * P)
            source = aspect_v[segments, :] if t == 0 else feature[segments, t - 1, :]
            nc.sync.dma_start(out=raw[g][:, t * K : (t + 1) * K], in_=source)

        load_w(0)
        nc.sync.dma_start(out=bias_row[0:1, :], in_=b.rearrange("(o m) -> o m", o=1))
        load_w(W_TILES_PER_LOAD)
        load_rows(0)
        for first in range(W_TILES_PER_HALF, W_TILES, W_TILES_PER_LOAD):
            load_w(first)
        for i in range(1, ROW_TILES):
            load_rows(i)

        def transpose_rows(words, bank):
            for j in range(WORDS // P):
                cols = slice(j * P, (j + 1) * P)
                nc.tensor.transpose(bank[:, cols], words[:, cols], identity[:])

        def pairs_side_by_side(bank):
            return bank.rearrange("p (c u r) -> p c r u", c=PASSES, u=2)

        bias = const.tile([P, M], F32)
        for h in range(HALVES):
            half = slice(h * BANK, (h + 1) * BANK)
            b_bank = psum_y.tile([P, BANK], F32, name="y")
            nc.tensor.matmul(out=b_bank[:], lhsT=ones[:], rhs=bias_row[:, half], start=True, stop=True)
            nc.vector.tensor_copy(out=bias[:, half], in_=b_bank[:])

        w_grouped = const.tile([P, PASSES * M * 4], BF16, align_bytes=64)
        w_grouped_words = w_grouped[:].bitcast(F32).rearrange(
            "p (c m u) -> p c m u", c=PASSES, u=2
        )
        w_codes = const.tile([P, PASSES * M], U32, align_bytes=64)
        w_scales = const.tile([P, PASSES * M], U8, align_bytes=64)
        w_words = w_raw[:].bitcast(F32)
        for wt in range(W_TILES):
            w_bank = psum_y.tile([P, BANK], F32, name="y")
            transpose_rows(w_words[:, wt * WORDS : (wt + 1) * WORDS], w_bank)
            target = w_grouped_words[:, :, wt * P : (wt + 1) * P, :]
            if wt % 2 == 0:
                nc.scalar.copy(out=target, in_=pairs_side_by_side(w_bank))
            else:
                nc.vector.tensor_copy(out=target, in_=pairs_side_by_side(w_bank))
            if (wt + 1) % W_TILES_PER_HALF == 0:
                h = wt // W_TILES_PER_HALF
                for c in range(PASSES):
                    lo = c * M + h * BANK
                    nc.vector.quantize_mx(
                        out=w_codes[:, lo : lo + BANK].bitcast(FP8X4),
                        scales=w_scales[:, lo : lo + BANK],
                        in_=w_grouped[:, 4 * lo : 4 * (lo + BANK)],
                    )

        grouped = {}
        codes = {}
        scales = {}
        z = {}
        sumsq = {}
        rnorm = {}
        fm = {}

        def transpose_and_regroup(i):
            g, t = divmod(i, TILES_PER_GROUP)
            x_bank = psum_t.tile([P, BANK], F32, name="xt")
            transpose_rows(raw[g][:].bitcast(F32)[:, t * WORDS : (t + 1) * WORDS], x_bank)
            grouped[i] = grouped_pool.tile([P, 2 * WORDS], BF16, name="grouped", align_bytes=64)
            nc.scalar.copy(
                out=grouped[i][:].bitcast(F32).rearrange("p (c r u) -> p c r u", c=PASSES, u=2),
                in_=pairs_side_by_side(x_bank),
            )

        def quantise(i):
            codes[i] = mx_pool.tile([P, PASSES * P], U32, name="codes", align_bytes=64)
            scales[i] = mx_pool.tile([P, PASSES * P], U8, name="scales", align_bytes=64)
            nc.vector.quantize_mx(
                out=codes[i][:].bitcast(FP8X4), scales=scales[i][:], in_=grouped[i][:]
            )

        def multiply_and_add_bias(i):
            z[i] = z_pool.tile([P, M], F32, name="z")
            for h in range(HALVES):
                y = psum_y.tile([P, BANK], F32, name="y")
                for c in range(PASSES):
                    x_cols = slice(c * P, (c + 1) * P)
                    w_cols = slice(c * M + h * BANK, c * M + (h + 1) * BANK)
                    nc.tensor.matmul_mx(
                        out=y[:],
                        lhsT=codes[i][:, x_cols].bitcast(FP8X4),
                        lhsT_scale=scales[i][:, x_cols],
                        rhs=w_codes[:, w_cols].bitcast(FP8X4),
                        rhs_scale=w_scales[:, w_cols],
                        start=(c == 0),
                        stop=(c == PASSES - 1),
                    )
                half = slice(h * BANK, (h + 1) * BANK)
                nc.vector.tensor_tensor(out=z[i][:, half], in0=y[:], in1=bias[:, half], op=ALU.add)

        def sum_of_squares(i):
            sumsq[i] = norm_pool.tile([P, 1], F32, name="sumsq")
            squares = scratch_pool.tile([P, M], F32, name="squares")
            nc.scalar.activation(out=squares[:], in_=z[i][:], func=ACT.Square, accum_out=sumsq[i][:])

        def reciprocal_norm(i):
            t = i % TILES_PER_GROUP
            clamped = norm_pool.tile([P, 1], F32, name="clamped")
            nc.gpsimd.tensor_scalar(
                out=clamped[:], in0=sumsq[i][:], scalar1=1e-24,
                scalar2=(1.0 if t == 0 else float(TOKENS * TOKENS)), op0=ALU.max, op1=ALU.mult,
            )
            rnorm[i] = norm_pool.tile([P, 1], F32, name="rnorm")
            nc.gpsimd.tensor_tensor(out=rnorm[i][:], in0=clamped[:], in1=minus_half[:], op=ALU.pow)

        def normalise_alone(i):
            g, t = divmod(i, TILES_PER_GROUP)
            if t == 0:
                q = out_pool.tile([P, M], F32, name="q")
                nc.scalar.activation(out=q[:], in_=z[i][:], func=ACT.Copy, scale=rnorm[i][:])
                nc.sync.dma_start(out=out_0[g * P : (g + 1) * P, :], in_=q[:])
            if t == 1:
                fm[g] = out_pool.tile([P, M], F32, name="fm")
                nc.scalar.activation(out=fm[g][:], in_=z[i][:], func=ACT.Copy, scale=rnorm[i][:])

        def add_to_mean(i):
            g, t = divmod(i, TILES_PER_GROUP)
            if t >= 2:
                nc.vector.scalar_tensor_tensor(
                    out=fm[g][:], in0=z[i][:], scalar=rnorm[i][:], in1=fm[g][:],
                    op0=ALU.mult, op1=ALU.add,
                )
            if t == TILES_PER_GROUP - 1:
                nc.sync.dma_start(out=out_1[g * P : (g + 1) * P, :], in_=fm[g][:])

        for step in range(-AHEAD_TRANSPOSE, ROW_TILES + BEHIND_MEAN):
            if 0 <= step < ROW_TILES:
                multiply_and_add_bias(step)
            if step + AHEAD_TRANSPOSE < ROW_TILES:
                transpose_and_regroup(step + AHEAD_TRANSPOSE)
            if 0 <= step + AHEAD_QUANTISE < ROW_TILES:
                quantise(step + AHEAD_QUANTISE)
            if 0 <= step - BEHIND_NORM < ROW_TILES:
                sum_of_squares(step - BEHIND_NORM)
                reciprocal_norm(step - BEHIND_NORM)
            if 0 <= step - BEHIND_SCALE < ROW_TILES:
                normalise_alone(step - BEHIND_SCALE)
            if 0 <= step - BEHIND_MEAN < ROW_TILES:
                add_to_mean(step - BEHIND_MEAN)
